import numpy as np
import ml_dtypes

BF16 = ml_dtypes.bfloat16


def bf(x):
    return np.asarray(x, np.float32).astype(BF16)


def f32(x):
    return np.asarray(x, np.float32)


def f64(x):
    return np.asarray(x).astype(np.float64)


def striped(idx):
    return np.tile(idx.reshape(-1, 16).T, (8, 1))


NB, D, C, S, N = 2, 128, 256, 2048, 256
MOM = 0.5


def unit(a):
    a = a.reshape(NB, D, -1)
    return (a / np.sqrt((a * a).sum(axis=1, keepdims=True))).reshape(C, -1)


def setup_inputs():
    return {"base": f32(unit(np.random.uniform(-1.0, 1.0, (C, S)))), "old": f32(unit(np.random.uniform(-1.0, 1.0, (C, N)))), "v": f32(np.random.standard_normal((C, N))), "offs": striped(np.random.permutation(S)[:N])}


def reference(base, old, v, offs):
    idx = offs[:16].T.reshape(-1)
    p = (f64(old) * MOM + f64(v) * (1.0 - MOM)).reshape(NB, D, N)
    r = 1.0 / np.sqrt((p * p).sum(axis=1, keepdims=True))
    out = f64(base).copy()
    out[:, idx] = (p * r).reshape(C, N)
    return out

@@ -1,0 +1,57 @@
+import concourse.mybir as mybir
+
+FP32 = mybir.dt.float32
+BF16 = mybir.dt.bfloat16
+U16 = mybir.dt.uint16
+ADD = mybir.AluOpType.add
+MULT = mybir.AluOpType.mult
+SQRT = mybir.ActivationFunctionType.Sqrt
+
+BANKS = 2
+FEATURES = 128
+ENTRIES = 2048
+LISTED = 256
+
+FLOPS = 2 * BANKS * FEATURES * LISTED
+
+
+def tile_contrastmemory_s_kernel(tc, base, old, v, offs, out):
+    nc = tc.nc
+    with (
+        tc.tile_pool(name="held", bufs=1) as held,
+        tc.tile_pool(name="banks", bufs=BANKS) as banks,
+        tc.psum_pool(name="psum", bufs=BANKS) as psum,
+    ):
+        offsets = held.tile([FEATURES, LISTED // 16], U16, name="offsets")
+        nc.sync.dma_start(offsets[:], offs)
+
+        ones = held.tile([FEATURES, FEATURES], BF16, name="ones")
+        nc.gpsimd.memset(ones[:], 1.0)
+
+        for b in range(BANKS):
+            rows = slice(b * FEATURES, (b + 1) * FEATURES)
+
+            old_t = banks.tile([FEATURES, LISTED], FP32, name="old_t")
+            nc.sync.dma_start(old_t[:], old[rows, :])
+            v_t = banks.tile([FEATURES, LISTED], FP32, name="v_t")
+            nc.sync.dma_start(v_t[:], v[rows, :])
+            window = banks.tile([FEATURES, ENTRIES], FP32, name="window")
+            nc.sync.dma_start(window[:], base[rows, :])
+
+            both = banks.tile([FEATURES, LISTED], FP32, name="both")
+            nc.vector.tensor_tensor(both[:], old_t[:], v_t[:], ADD)
+            p = banks.tile([FEATURES, LISTED], FP32, name="p")
+            nc.vector.tensor_scalar(p[:], both[:], 0.5, None, MULT)
+
+            squares = banks.tile([FEATURES, LISTED], BF16, name="squares")
+            nc.vector.tensor_tensor(squares[:], p[:], p[:], MULT)
+            sums = psum.tile([FEATURES, LISTED], FP32, name="sums")
+            nc.tensor.matmul(sums[:], ones[:], squares[:], start=True, stop=True)
+
+            norm = banks.tile([FEATURES, LISTED], FP32, name="norm")
+            nc.scalar.activation(norm[:], sums[:], SQRT)
+            r = banks.tile([FEATURES, LISTED], FP32, name="r")
+            nc.vector.reciprocal(r[:], norm[:])
+
+            nc.vector.tensor_tensor(window[:].indirect(offsets[:]), p[:], r[:], MULT)
+            nc.sync.dma_start(out[rows, :], window[:])

@@ -5,7 +5,7 @@ BF16 = mybir.dt.bfloat16
 U16 = mybir.dt.uint16
 ADD = mybir.AluOpType.add
 MULT = mybir.AluOpType.mult
-SQRT = mybir.ActivationFunctionType.Sqrt
+RSQRT = mybir.ActivationFunctionType.Abs_reciprocal_sqrt
 
 BANKS = 2
 FEATURES = 128
@@ -48,10 +48,8 @@ def tile_contrastmemory_s_kernel(tc, base, old, v, offs, out):
             sums = psum.tile([FEATURES, LISTED], FP32, name="sums")
             nc.tensor.matmul(sums[:], ones[:], squares[:], start=True, stop=True)
 
-            norm = banks.tile([FEATURES, LISTED], FP32, name="norm")
-            nc.scalar.activation(norm[:], sums[:], SQRT)
             r = banks.tile([FEATURES, LISTED], FP32, name="r")
-            nc.vector.reciprocal(r[:], norm[:])
+            nc.scalar.activation(r[:], sums[:], RSQRT)
 
             nc.vector.tensor_tensor(window[:].indirect(offsets[:]), p[:], r[:], MULT)
             nc.sync.dma_start(out[rows, :], window[:])

@@ -17,39 +17,41 @@ FLOPS = 2 * BANKS * FEATURES * LISTED
 
 def tile_contrastmemory_s_kernel(tc, base, old, v, offs, out):
     nc = tc.nc
+    bank_rows = [slice(b * FEATURES, (b + 1) * FEATURES) for b in range(BANKS)]
     with (
         tc.tile_pool(name="held", bufs=1) as held,
-        tc.tile_pool(name="banks", bufs=BANKS) as banks,
-        tc.psum_pool(name="psum", bufs=BANKS) as psum,
+        tc.psum_pool(name="psum", bufs=1) as psum,
     ):
         offsets = held.tile([FEATURES, LISTED // 16], U16, name="offsets")
         nc.sync.dma_start(offsets[:], offs)
+        old_t, v_t, window = [], [], []
+        for b in range(BANKS):
+            old_t.append(held.tile([FEATURES, LISTED], FP32, name=f"old_t{b}"))
+            nc.sync.dma_start(old_t[b][:], old[bank_rows[b], :])
+            v_t.append(held.tile([FEATURES, LISTED], FP32, name=f"v_t{b}"))
+            nc.sync.dma_start(v_t[b][:], v[bank_rows[b], :])
+        for b in range(BANKS):
+            window.append(held.tile([FEATURES, ENTRIES], FP32, name=f"window{b}"))
+            nc.sync.dma_start(window[b][:], base[bank_rows[b], :])
 
         ones = held.tile([FEATURES, FEATURES], BF16, name="ones")
         nc.gpsimd.memset(ones[:], 1.0)
 
+        p, r = [], []
         for b in range(BANKS):
-            rows = slice(b * FEATURES, (b + 1) * FEATURES)
+            both = held.tile([FEATURES, LISTED], FP32, name=f"both{b}")
+            nc.vector.tensor_tensor(both[:], old_t[b][:], v_t[b][:], ADD)
+            p.append(held.tile([FEATURES, LISTED], FP32, name=f"p{b}"))
+            nc.vector.tensor_scalar(p[b][:], both[:], 0.5, None, MULT)
 
-            old_t = banks.tile([FEATURES, LISTED], FP32, name="old_t")
-            nc.sync.dma_start(old_t[:], old[rows, :])
-            v_t = banks.tile([FEATURES, LISTED], FP32, name="v_t")
-            nc.sync.dma_start(v_t[:], v[rows, :])
-            window = banks.tile([FEATURES, ENTRIES], FP32, name="window")
-            nc.sync.dma_start(window[:], base[rows, :])
-
-            both = banks.tile([FEATURES, LISTED], FP32, name="both")
-            nc.vector.tensor_tensor(both[:], old_t[:], v_t[:], ADD)
-            p = banks.tile([FEATURES, LISTED], FP32, name="p")
-            nc.vector.tensor_scalar(p[:], both[:], 0.5, None, MULT)
-
-            squares = banks.tile([FEATURES, LISTED], BF16, name="squares")
-            nc.vector.tensor_tensor(squares[:], p[:], p[:], MULT)
-            sums = psum.tile([FEATURES, LISTED], FP32, name="sums")
+            squares = held.tile([FEATURES, LISTED], BF16, name=f"squares{b}")
+            nc.vector.tensor_tensor(squares[:], p[b][:], p[b][:], MULT)
+            sums = psum.tile([FEATURES, LISTED], FP32, name=f"sums{b}")
             nc.tensor.matmul(sums[:], ones[:], squares[:], start=True, stop=True)
 
-            r = banks.tile([FEATURES, LISTED], FP32, name="r")
-            nc.scalar.activation(r[:], sums[:], RSQRT)
+            r.append(held.tile([FEATURES, LISTED], FP32, name=f"r{b}"))
+            nc.scalar.activation(r[b][:], sums[:], RSQRT)
 
-            nc.vector.tensor_tensor(window[:].indirect(offsets[:]), p[:], r[:], MULT)
-            nc.sync.dma_start(out[rows, :], window[:])
+        for b in range(BANKS):
+            nc.vector.tensor_tensor(window[b][:].indirect(offsets[:]), p[b][:], r[b][:], MULT)
+            nc.sync.dma_start(out[bank_rows[b], :], window[b][:])

@@ -24,12 +24,11 @@ def tile_contrastmemory_s_kernel(tc, base, old, v, offs, out):
     ):
         offsets = held.tile([FEATURES, LISTED // 16], U16, name="offsets")
         nc.sync.dma_start(offsets[:], offs)
-        old_t, v_t, window = [], [], []
-        for b in range(BANKS):
-            old_t.append(held.tile([FEATURES, LISTED], FP32, name=f"old_t{b}"))
-            nc.sync.dma_start(old_t[b][:], old[bank_rows[b], :])
-            v_t.append(held.tile([FEATURES, LISTED], FP32, name=f"v_t{b}"))
-            nc.sync.dma_start(v_t[b][:], v[bank_rows[b], :])
+        old_t = held.tile([FEATURES, BANKS, LISTED], FP32, name="old_t")
+        nc.sync.dma_start(old_t[:], old.rearrange("(b d) n -> d b n", b=BANKS))
+        v_t = held.tile([FEATURES, BANKS, LISTED], FP32, name="v_t")
+        nc.sync.dma_start(v_t[:], v.rearrange("(b d) n -> d b n", b=BANKS))
+        window = []
         for b in range(BANKS):
             window.append(held.tile([FEATURES, ENTRIES], FP32, name=f"window{b}"))
             nc.sync.dma_start(window[b][:], base[bank_rows[b], :])
@@ -40,7 +39,7 @@ def tile_contrastmemory_s_kernel(tc, base, old, v, offs, out):
         p, r = [], []
         for b in range(BANKS):
             both = held.tile([FEATURES, LISTED], FP32, name=f"both{b}")
-            nc.vector.tensor_tensor(both[:], old_t[b][:], v_t[b][:], ADD)
+            nc.vector.tensor_tensor(both[:], old_t[:, b, :], v_t[:, b, :], ADD)
             p.append(held.tile([FEATURES, LISTED], FP32, name=f"p{b}"))
             nc.vector.tensor_scalar(p[b][:], both[:], 0.5, None, MULT)
 

@@ -36,20 +36,22 @@ def tile_contrastmemory_s_kernel(tc, base, old, v, offs, out):
         ones = held.tile([FEATURES, FEATURES], BF16, name="ones")
         nc.gpsimd.memset(ones[:], 1.0)
 
-        p, r = [], []
+        total, r = [], []
         for b in range(BANKS):
-            both = held.tile([FEATURES, LISTED], FP32, name=f"both{b}")
-            nc.vector.tensor_tensor(both[:], old_t[:, b, :], v_t[:, b, :], ADD)
-            p.append(held.tile([FEATURES, LISTED], FP32, name=f"p{b}"))
-            nc.vector.tensor_scalar(p[b][:], both[:], 0.5, None, MULT)
-
+            total.append(held.tile([FEATURES, LISTED], FP32, name=f"total{b}"))
+            nc.vector.tensor_tensor(total[b][:], old_t[:, b, :], v_t[:, b, :], ADD)
             squares = held.tile([FEATURES, LISTED], BF16, name=f"squares{b}")
-            nc.vector.tensor_tensor(squares[:], p[b][:], p[b][:], MULT)
+            nc.vector.tensor_tensor(squares[:], total[b][:], total[b][:], MULT)
             sums = psum.tile([FEATURES, LISTED], FP32, name=f"sums{b}")
             nc.tensor.matmul(sums[:], ones[:], squares[:], start=True, stop=True)
 
             r.append(held.tile([FEATURES, LISTED], FP32, name=f"r{b}"))
-            nc.scalar.activation(r[b][:], sums[:], RSQRT)
+            nc.scalar.activation(r[b][:], sums[:], RSQRT, scale=0.25)
+
+        p = []
+        for b in range(BANKS):
+            p.append(held.tile([FEATURES, LISTED], FP32, name=f"p{b}"))
+            nc.vector.tensor_scalar(p[b][:], total[b][:], 0.5, None, MULT)
 
         for b in range(BANKS):
             nc.vector.tensor_tensor(window[b][:].indirect(offsets[:]), p[b][:], r[b][:], MULT)

@@ -22,12 +22,12 @@ def tile_contrastmemory_s_kernel(tc, base, old, v, offs, out):
         tc.tile_pool(name="held", bufs=1) as held,
         tc.psum_pool(name="psum", bufs=1) as psum,
     ):
-        offsets = held.tile([FEATURES, LISTED // 16], U16, name="offsets")
-        nc.sync.dma_start(offsets[:], offs)
         old_t = held.tile([FEATURES, BANKS, LISTED], FP32, name="old_t")
         nc.sync.dma_start(old_t[:], old.rearrange("(b d) n -> d b n", b=BANKS))
         v_t = held.tile([FEATURES, BANKS, LISTED], FP32, name="v_t")
         nc.sync.dma_start(v_t[:], v.rearrange("(b d) n -> d b n", b=BANKS))
+        offsets = held.tile([FEATURES, LISTED // 16], U16, name="offsets")
+        nc.sync.dma_start(offsets[:], offs)
         window = []
         for b in range(BANKS):
             window.append(held.tile([FEATURES, ENTRIES], FP32, name=f"window{b}"))

@@ -7,52 +7,59 @@ ADD = mybir.AluOpType.add
 MULT = mybir.AluOpType.mult
 RSQRT = mybir.ActivationFunctionType.Abs_reciprocal_sqrt
 
-BANKS = 2
-FEATURES = 128
+PARTITIONS = 128
+CHANNELS = 256
+PAIR = CHANNELS // PARTITIONS
+BANK_PARTITIONS = PARTITIONS // 2
 ENTRIES = 2048
 LISTED = 256
 
-FLOPS = 2 * BANKS * FEATURES * LISTED
+FLOPS = 2 * CHANNELS * LISTED
 
 
 def tile_contrastmemory_s_kernel(tc, base, old, v, offs, out):
     nc = tc.nc
-    bank_rows = [slice(b * FEATURES, (b + 1) * FEATURES) for b in range(BANKS)]
+    old_pairs = old.rearrange("(q w) n -> q w n", w=PAIR)
+    v_pairs = v.rearrange("(q w) n -> q w n", w=PAIR)
+    base_pairs = base.rearrange("(q w) s -> q w s", w=PAIR)
+    out_pairs = out.rearrange("(q w) s -> q w s", w=PAIR)
     with (
         tc.tile_pool(name="held", bufs=1) as held,
         tc.psum_pool(name="psum", bufs=1) as psum,
     ):
-        old_t = held.tile([FEATURES, BANKS, LISTED], FP32, name="old_t")
-        nc.sync.dma_start(old_t[:], old.rearrange("(b d) n -> d b n", b=BANKS))
-        v_t = held.tile([FEATURES, BANKS, LISTED], FP32, name="v_t")
-        nc.sync.dma_start(v_t[:], v.rearrange("(b d) n -> d b n", b=BANKS))
-        offsets = held.tile([FEATURES, LISTED // 16], U16, name="offsets")
+        old_t = held.tile([PARTITIONS, PAIR, LISTED], FP32, name="old_t")
+        nc.sync.dma_start(old_t[:], old_pairs)
+        v_t = held.tile([PARTITIONS, PAIR, LISTED], FP32, name="v_t")
+        nc.sync.dma_start(v_t[:], v_pairs)
+        offsets = held.tile([PARTITIONS, LISTED // 16], U16, name="offsets")
         nc.sync.dma_start(offsets[:], offs)
         window = []
-        for b in range(BANKS):
-            window.append(held.tile([FEATURES, ENTRIES], FP32, name=f"window{b}"))
-            nc.sync.dma_start(window[b][:], base[bank_rows[b], :])
+        for w in range(PAIR):
+            window.append(held.tile([PARTITIONS, ENTRIES], FP32, name=f"window{w}"))
+            nc.sync.dma_start(window[w][:], base_pairs[:, w, :])
 
-        ones = held.tile([FEATURES, FEATURES], BF16, name="ones")
-        nc.gpsimd.memset(ones[:], 1.0)
+        same_bank = held.tile([PARTITIONS, PARTITIONS], BF16, name="same_bank")
+        nc.gpsimd.memset(same_bank[:], 0.0)
+        for first in range(0, PARTITIONS, BANK_PARTITIONS):
+            block = slice(first, first + BANK_PARTITIONS)
+            nc.gpsimd.memset(same_bank[block, block], 1.0)
 
-        total, r = [], []
-        for b in range(BANKS):
-            total.append(held.tile([FEATURES, LISTED], FP32, name=f"total{b}"))
-            nc.vector.tensor_tensor(total[b][:], old_t[:, b, :], v_t[:, b, :], ADD)
-            squares = held.tile([FEATURES, LISTED], BF16, name=f"squares{b}")
-            nc.vector.tensor_tensor(squares[:], total[b][:], total[b][:], MULT)
-            sums = psum.tile([FEATURES, LISTED], FP32, name=f"sums{b}")
-            nc.tensor.matmul(sums[:], ones[:], squares[:], start=True, stop=True)
+        total = held.tile([PARTITIONS, PAIR, LISTED], FP32, name="total")
+        squares = held.tile([PARTITIONS, PAIR, LISTED], BF16, name="squares")
+        sums = psum.tile([PARTITIONS, LISTED], FP32, name="sums")
+        for w in range(PAIR):
+            nc.vector.tensor_tensor(total[:, w, :], old_t[:, w, :], v_t[:, w, :], ADD)
+            nc.vector.tensor_tensor(squares[:, w, :], total[:, w, :], total[:, w, :], MULT)
+            nc.tensor.matmul(
+                sums[:], same_bank[:], squares[:, w, :], start=(w == 0), stop=(w == PAIR - 1)
+            )
 
-            r.append(held.tile([FEATURES, LISTED], FP32, name=f"r{b}"))
-            nc.scalar.activation(r[b][:], sums[:], RSQRT, scale=0.25)
+        r = held.tile([PARTITIONS, LISTED], FP32, name="r")
+        nc.scalar.activation(r[:], sums[:], RSQRT, scale=0.25)
 
-        p = []
-        for b in range(BANKS):
-            p.append(held.tile([FEATURES, LISTED], FP32, name=f"p{b}"))
-            nc.vector.tensor_scalar(p[b][:], total[b][:], 0.5, None, MULT)
+        p = held.tile([PARTITIONS, PAIR, LISTED], FP32, name="p")
+        nc.vector.tensor_scalar(p[:], total[:], 0.5, None, MULT)
 
-        for b in range(BANKS):
-            nc.vector.tensor_tensor(window[b][:].indirect(offsets[:]), p[b][:], r[b][:], MULT)
-            nc.sync.dma_start(out[bank_rows[b], :], window[b][:])
+        for w in range(PAIR):
+            nc.vector.tensor_tensor(window[w][:].indirect(offsets[:]), p[:, w, :], r[:], MULT)
+            nc.sync.dma_start(out_pairs[:, w, :], window[w][:])

@@ -54,12 +54,11 @@ def tile_contrastmemory_s_kernel(tc, base, old, v, offs, out):
                 sums[:], same_bank[:], squares[:, w, :], start=(w == 0), stop=(w == PAIR - 1)
             )
 
-        r = held.tile([PARTITIONS, LISTED], FP32, name="r")
-        nc.scalar.activation(r[:], sums[:], RSQRT, scale=0.25)
-
-        p = held.tile([PARTITIONS, PAIR, LISTED], FP32, name="p")
-        nc.vector.tensor_scalar(p[:], total[:], 0.5, None, MULT)
+        half_r = held.tile([PARTITIONS, LISTED], FP32, name="half_r")
+        nc.scalar.activation(half_r[:], sums[:], RSQRT)
 
         for w in range(PAIR):
-            nc.vector.tensor_tensor(window[w][:].indirect(offsets[:]), p[:, w, :], r[:], MULT)
+            nc.vector.tensor_tensor(
+                window[w][:].indirect(offsets[:]), total[:, w, :], half_r[:], MULT
+            )
             nc.sync.dma_start(out_pairs[:, w, :], window[w][:])

@@ -13,6 +13,7 @@ PAIR = CHANNELS // PARTITIONS
 BANK_PARTITIONS = PARTITIONS // 2
 ENTRIES = 2048
 LISTED = 256
+AXI_BURST = 256
 
 FLOPS = 2 * CHANNELS * LISTED
 
@@ -35,7 +36,9 @@ def tile_contrastmemory_s_kernel(tc, base, old, v, offs, out):
         nc.sync.dma_start(offsets[:], offs)
         window = []
         for w in range(PAIR):
-            window.append(held.tile([PARTITIONS, ENTRIES], FP32, name=f"window{w}"))
+            window.append(
+                held.tile([PARTITIONS, ENTRIES], FP32, name=f"window{w}", align_bytes=AXI_BURST)
+            )
             nc.sync.dma_start(window[w][:], base_pairs[:, w, :])
 
         same_bank = held.tile([PARTITIONS, PARTITIONS], BF16, name="same_bank")

@@ -42,10 +42,10 @@ def tile_contrastmemory_s_kernel(tc, base, old, v, offs, out):
             nc.sync.dma_start(window[w][:], base_pairs[:, w, :])
 
         same_bank = held.tile([PARTITIONS, PARTITIONS], BF16, name="same_bank")
-        nc.gpsimd.memset(same_bank[:], 0.0)
+        nc.vector.memset(same_bank[:], 0.0)
         for first in range(0, PARTITIONS, BANK_PARTITIONS):
             block = slice(first, first + BANK_PARTITIONS)
-            nc.gpsimd.memset(same_bank[block, block], 1.0)
+            nc.vector.memset(same_bank[block, block], 1.0)
 
         total = held.tile([PARTITIONS, PAIR, LISTED], FP32, name="total")
         squares = held.tile([PARTITIONS, PAIR, LISTED], BF16, name="squares")

@@ -13,6 +13,7 @@ PAIR = CHANNELS // PARTITIONS
 BANK_PARTITIONS = PARTITIONS // 2
 ENTRIES = 2048
 LISTED = 256
+LAST_PIECE = LISTED // 4
 AXI_BURST = 256
 
 FLOPS = 2 * CHANNELS * LISTED
@@ -50,11 +51,18 @@ def tile_contrastmemory_s_kernel(tc, base, old, v, offs, out):
         total = held.tile([PARTITIONS, PAIR, LISTED], FP32, name="total")
         squares = held.tile([PARTITIONS, PAIR, LISTED], BF16, name="squares")
         sums = psum.tile([PARTITIONS, LISTED], FP32, name="sums")
-        for w in range(PAIR):
-            nc.vector.tensor_tensor(total[:, w, :], old_t[:, w, :], v_t[:, w, :], ADD)
-            nc.vector.tensor_tensor(squares[:, w, :], total[:, w, :], total[:, w, :], MULT)
+        nc.vector.tensor_tensor(total[:, 0, :], old_t[:, 0, :], v_t[:, 0, :], ADD)
+        nc.vector.tensor_tensor(squares[:, 0, :], total[:, 0, :], total[:, 0, :], MULT)
+        nc.tensor.matmul(sums[:], same_bank[:], squares[:, 0, :], start=True, stop=False)
+        nc.vector.tensor_tensor(total[:, 1, :], old_t[:, 1, :], v_t[:, 1, :], ADD)
+        for piece in (slice(0, LISTED - LAST_PIECE), slice(LISTED - LAST_PIECE, LISTED)):
+            nc.vector.tensor_tensor(squares[:, 1, piece], total[:, 1, piece], total[:, 1, piece], MULT)
             nc.tensor.matmul(
-                sums[:], same_bank[:], squares[:, w, :], start=(w == 0), stop=(w == PAIR - 1)
+                sums[:, piece],
+                same_bank[:],
+                squares[:, 1, piece],
+                start=False,
+                stop=(piece.stop == LISTED),
             )
 
         half_r = held.tile([PARTITIONS, LISTED], FP32, name="half_r")

@@ -6,6 +6,7 @@ U16 = mybir.dt.uint16
 ADD = mybir.AluOpType.add
 MULT = mybir.AluOpType.mult
 RSQRT = mybir.ActivationFunctionType.Abs_reciprocal_sqrt
+SQUARE = mybir.ActivationFunctionType.Square
 
 PARTITIONS = 128
 CHANNELS = 256
@@ -13,7 +14,7 @@ PAIR = CHANNELS // PARTITIONS
 BANK_PARTITIONS = PARTITIONS // 2
 ENTRIES = 2048
 LISTED = 256
-LAST_PIECE = LISTED // 4
+HALF = LISTED // 2
 AXI_BURST = 256
 
 FLOPS = 2 * CHANNELS * LISTED
@@ -48,25 +49,28 @@ def tile_contrastmemory_s_kernel(tc, base, old, v, offs, out):
             block = slice(first, first + BANK_PARTITIONS)
             nc.vector.memset(same_bank[block, block], 1.0)
 
+        warm_in = held.tile([PARTITIONS, 1], FP32, name="warm_in")
+        warm_out = held.tile([PARTITIONS, 1], FP32, name="warm_out")
+        nc.vector.memset(warm_in[:], 1.0)
+        nc.scalar.activation(warm_out[:], warm_in[:], RSQRT)
+
         total = held.tile([PARTITIONS, PAIR, LISTED], FP32, name="total")
         squares = held.tile([PARTITIONS, PAIR, LISTED], BF16, name="squares")
-        sums = psum.tile([PARTITIONS, LISTED], FP32, name="sums")
-        nc.vector.tensor_tensor(total[:, 0, :], old_t[:, 0, :], v_t[:, 0, :], ADD)
-        nc.vector.tensor_tensor(squares[:, 0, :], total[:, 0, :], total[:, 0, :], MULT)
-        nc.tensor.matmul(sums[:], same_bank[:], squares[:, 0, :], start=True, stop=False)
-        nc.vector.tensor_tensor(total[:, 1, :], old_t[:, 1, :], v_t[:, 1, :], ADD)
-        for piece in (slice(0, LISTED - LAST_PIECE), slice(LISTED - LAST_PIECE, LISTED)):
-            nc.vector.tensor_tensor(squares[:, 1, piece], total[:, 1, piece], total[:, 1, piece], MULT)
-            nc.tensor.matmul(
-                sums[:, piece],
-                same_bank[:],
-                squares[:, 1, piece],
-                start=False,
-                stop=(piece.stop == LISTED),
-            )
+        halves = (slice(0, HALF), slice(HALF, LISTED))
+        sums = []
+        for h, half in enumerate(halves):
+            nc.vector.tensor_tensor(total[:, :, half], old_t[:, :, half], v_t[:, :, half], ADD)
+            nc.scalar.activation(squares[:, 1, half], total[:, 1, half], SQUARE)
+            nc.vector.tensor_tensor(squares[:, 0, half], total[:, 0, half], total[:, 0, half], MULT)
+            sums.append(psum.tile([PARTITIONS, HALF], FP32, name=f"sums{h}"))
+            for w in range(PAIR):
+                nc.tensor.matmul(
+                    sums[h][:], same_bank[:], squares[:, w, half], start=(w == 0), stop=(w == PAIR - 1)
+                )
 
         half_r = held.tile([PARTITIONS, LISTED], FP32, name="half_r")
-        nc.scalar.activation(half_r[:], sums[:], RSQRT)
+        for h, half in enumerate(halves):
+            nc.scalar.activation(half_r[:, half], sums[h][:], RSQRT)
 
         for w in range(PAIR):
             nc.vector.tensor_tensor(

@@ -6,7 +6,6 @@ U16 = mybir.dt.uint16
 ADD = mybir.AluOpType.add
 MULT = mybir.AluOpType.mult
 RSQRT = mybir.ActivationFunctionType.Abs_reciprocal_sqrt
-SQUARE = mybir.ActivationFunctionType.Square
 
 PARTITIONS = 128
 CHANNELS = 256
@@ -49,19 +48,13 @@ def tile_contrastmemory_s_kernel(tc, base, old, v, offs, out):
             block = slice(first, first + BANK_PARTITIONS)
             nc.vector.memset(same_bank[block, block], 1.0)
 
-        warm_in = held.tile([PARTITIONS, 1], FP32, name="warm_in")
-        warm_out = held.tile([PARTITIONS, 1], FP32, name="warm_out")
-        nc.vector.memset(warm_in[:], 1.0)
-        nc.scalar.activation(warm_out[:], warm_in[:], RSQRT)
-
         total = held.tile([PARTITIONS, PAIR, LISTED], FP32, name="total")
         squares = held.tile([PARTITIONS, PAIR, LISTED], BF16, name="squares")
         halves = (slice(0, HALF), slice(HALF, LISTED))
         sums = []
         for h, half in enumerate(halves):
             nc.vector.tensor_tensor(total[:, :, half], old_t[:, :, half], v_t[:, :, half], ADD)
-            nc.scalar.activation(squares[:, 1, half], total[:, 1, half], SQUARE)
-            nc.vector.tensor_tensor(squares[:, 0, half], total[:, 0, half], total[:, 0, half], MULT)
+            nc.vector.tensor_tensor(squares[:, :, half], total[:, :, half], total[:, :, half], MULT)
             sums.append(psum.tile([PARTITIONS, HALF], FP32, name=f"sums{h}"))
             for w in range(PAIR):
                 nc.tensor.matmul(

@@ -33,14 +33,15 @@ def tile_contrastmemory_s_kernel(tc, base, old, v, offs, out):
         nc.sync.dma_start(old_t[:], old_pairs)
         v_t = held.tile([PARTITIONS, PAIR, LISTED], FP32, name="v_t")
         nc.sync.dma_start(v_t[:], v_pairs)
-        offsets = held.tile([PARTITIONS, LISTED // 16], U16, name="offsets")
-        nc.sync.dma_start(offsets[:], offs)
         window = []
         for w in range(PAIR):
             window.append(
                 held.tile([PARTITIONS, ENTRIES], FP32, name=f"window{w}", align_bytes=AXI_BURST)
             )
             nc.sync.dma_start(window[w][:], base_pairs[:, w, :])
+            if w == 0:
+                offsets = held.tile([PARTITIONS, LISTED // 16], U16, name="offsets")
+                nc.sync.dma_start(offsets[:], offs)
 
         same_bank = held.tile([PARTITIONS, PARTITIONS], BF16, name="same_bank")
         nc.vector.memset(same_bank[:], 0.0)

@@ -70,4 +70,8 @@ def tile_contrastmemory_s_kernel(tc, base, old, v, offs, out):
             nc.vector.tensor_tensor(
                 window[w][:].indirect(offsets[:]), total[:, w, :], half_r[:], MULT
             )
-            nc.sync.dma_start(out_pairs[:, w, :], window[w][:])
+            pieces = PAIR - w
+            columns = ENTRIES // pieces
+            for first in range(0, ENTRIES, columns):
+                piece = slice(first, first + columns)
+                nc.sync.dma_start(out_pairs[:, w, piece], window[w][:, piece])

import concourse.mybir as mybir

FP32 = mybir.dt.float32
BF16 = mybir.dt.bfloat16
U16 = mybir.dt.uint16
ADD = mybir.AluOpType.add
MULT = mybir.AluOpType.mult
RSQRT = mybir.ActivationFunctionType.Abs_reciprocal_sqrt

PARTITIONS = 128
CHANNELS = 256
PAIR = CHANNELS // PARTITIONS
BANK_PARTITIONS = PARTITIONS // 2
ENTRIES = 2048
LISTED = 256
HALF = LISTED // 2
AXI_BURST = 256

FLOPS = 2 * CHANNELS * LISTED


def tile_contrastmemory_s_kernel(tc, base, old, v, offs, out):
    nc = tc.nc
    old_pairs = old.rearrange("(q w) n -> q w n", w=PAIR)
    v_pairs = v.rearrange("(q w) n -> q w n", w=PAIR)
    base_pairs = base.rearrange("(q w) s -> q w s", w=PAIR)
    out_pairs = out.rearrange("(q w) s -> q w s", w=PAIR)
    with (
        tc.tile_pool(name="held", bufs=1) as held,
        tc.psum_pool(name="psum", bufs=1) as psum,
    ):
        old_t = held.tile([PARTITIONS, PAIR, LISTED], FP32, name="old_t")
        nc.sync.dma_start(old_t[:], old_pairs)
        v_t = held.tile([PARTITIONS, PAIR, LISTED], FP32, name="v_t")
        nc.sync.dma_start(v_t[:], v_pairs)
        window = []
        for w in range(PAIR):
            window.append(
                held.tile([PARTITIONS, ENTRIES], FP32, name=f"window{w}", align_bytes=AXI_BURST)
            )
            nc.sync.dma_start(window[w][:], base_pairs[:, w, :])
            if w == 0:
                offsets = held.tile([PARTITIONS, LISTED // 16], U16, name="offsets")
                nc.sync.dma_start(offsets[:], offs)

        same_bank = held.tile([PARTITIONS, PARTITIONS], BF16, name="same_bank")
        nc.vector.memset(same_bank[:], 0.0)
        for first in range(0, PARTITIONS, BANK_PARTITIONS):
            block = slice(first, first + BANK_PARTITIONS)
            nc.vector.memset(same_bank[block, block], 1.0)

        total = held.tile([PARTITIONS, PAIR, LISTED], FP32, name="total")
        squares = held.tile([PARTITIONS, PAIR, LISTED], BF16, name="squares")
        halves = (slice(0, HALF), slice(HALF, LISTED))
        sums = []
        for h, half in enumerate(halves):
            nc.vector.tensor_tensor(total[:, :, half], old_t[:, :, half], v_t[:, :, half], ADD)
            nc.vector.tensor_tensor(squares[:, :, half], total[:, :, half], total[:, :, half], MULT)
            sums.append(psum.tile([PARTITIONS, HALF], FP32, name=f"sums{h}"))
            for w in range(PAIR):
                nc.tensor.matmul(
                    sums[h][:], same_bank[:], squares[:, w, half], start=(w == 0), stop=(w == PAIR - 1)
                )

        half_r = held.tile([PARTITIONS, LISTED], FP32, name="half_r")
        for h, half in enumerate(halves):
            nc.scalar.activation(half_r[:, half], sums[h][:], RSQRT)

        for w in range(PAIR):
            nc.vector.tensor_tensor(
                window[w][:].indirect(offsets[:]), total[:, w, :], half_r[:], MULT
            )
            pieces = PAIR - w
            columns = ENTRIES // pieces
            for first in range(0, ENTRIES, columns):
                piece = slice(first, first + columns)
                nc.sync.dma_start(out_pairs[:, w, piece], window[w][:, piece])
